import numpy as np
import ml_dtypes


def mxq(x, axis, fmt="e4m3"):
    dtype, down = {"e4m3": (ml_dtypes.float8_e4m3fn, 7), "e5m2": (ml_dtypes.float8_e5m2, 14)}[fmt]
    v = np.moveaxis(np.asarray(x, np.float32).astype(ml_dtypes.bfloat16).astype(np.float64), axis, -1)
    blocks = v.reshape(v.shape[:-1] + (-1, 32))
    amax = np.abs(blocks).max(-1, keepdims=True)
    byte = np.maximum(np.where(amax > 0, np.frexp(amax)[1] - 1 + 127, 0) - down, 1)
    scale = np.exp2(byte - 127.0)
    codes = (blocks / scale).astype(np.float32).astype(dtype).astype(np.float64)
    return np.moveaxis((codes * scale).reshape(v.shape), -1, axis)


WIDE = False


def mx_kscale(k):
    if not WIDE:
        return np.ones(k)
    levels = np.array([10, -10, 5, -5, 0])
    a = np.random.permutation(np.resize(levels, k // 512 * 4)).reshape(k // 512, 4)
    idx = np.arange(k)
    return np.exp2(a[idx // 512, idx % 128 // 32])


BF16 = ml_dtypes.bfloat16


def bf(x):
    return np.asarray(x, np.float32).astype(BF16)


def f64(x):
    return np.asarray(x).astype(np.float64)


E2M1 = np.array([0.0, 0.5, 1.0, 1.5, 2.0, 3.0, 4.0, 6.0, -0.0, -0.5, -1.0, -1.5, -2.0, -3.0, -4.0, -6.0])


def pack_weight(w, fmt):
    k, n = w.shape
    w = f64(bf(w)).reshape(k // 32, 32, n)
    amax = np.abs(w).max(1)
    if fmt == "e4m3":
        byte = np.frexp(amax)[1] - 1 + 127 - 7
    else:
        mant, ex = np.frexp(amax / 6.0)
        byte = np.where(mant > 0.5, ex, ex - 1) + 127
    byte = np.clip(np.where(amax > 0, byte, 1), 1, 254)
    scaled = (w * np.exp2(127.0 - byte)[:, None, :]).reshape(k, n).astype(np.float32)
    by_word = np.ascontiguousarray(scaled.reshape(k // 512, 128, 4, n).transpose(0, 1, 3, 2))
    if fmt == "e4m3":
        words = by_word.astype(ml_dtypes.float8_e4m3fn).view(np.uint8)
    else:
        c = by_word.astype(ml_dtypes.float4_e2m1fn).view(np.uint8) & 0xF
        words = c[..., 0::2] | (c[..., 1::2] << 4)
    return np.ascontiguousarray(words), np.ascontiguousarray(byte.astype(np.uint8).reshape(k // 512, 16, n))


def unpack_weight(words, scales, fmt):
    g, p, n, _ = words.shape
    if fmt == "e4m3":
        vals = np.ascontiguousarray(words).view(ml_dtypes.float8_e4m3fn).astype(np.float64)
    else:
        nib = np.empty((g, p, n, 4), np.uint8)
        nib[..., 0::2] = words & 0xF
        nib[..., 1::2] = words >> 4
        vals = E2M1[nib]
    vals = vals * np.repeat(np.exp2(scales.astype(np.float64) - 127.0), 8, axis=1)[..., None]
    return vals.transpose(0, 1, 3, 2).reshape(g * 512, n)


B, IN, HID, BLK, OUT = 4096, 512, 1024, 512, 10
NB = HID // BLK


def setup_inputs():
    s = mx_kscale(IN)
    t = np.tile(mx_kscale(BLK), NB)
    x = bf(np.random.standard_normal((B, IN)) * s)
    W1 = np.random.standard_normal((HID, IN)) / np.sqrt(IN) / s * t[:, None]
    W1_words, W1_scales = pack_weight(np.ascontiguousarray(W1.T), "e4m3")
    return {
        "x": x,
        "W1_words": W1_words,
        "W1_scales": W1_scales,
        "b1": bf(np.random.standard_normal(HID) * 0.3 * t),
        "Wb": bf(np.random.standard_normal((NB, BLK, BLK)) * 1.4 / np.sqrt(BLK) / t.reshape(NB, 1, BLK)),
        "bb": bf(np.random.standard_normal(HID) * 0.3),
    }


def reference(x, W1_words, W1_scales, b1, Wb, bb):
    h = np.maximum((mxq(f64(x), 1, "e4m3") @ unpack_weight(W1_words, W1_scales, "e4m3")) + f64(b1), 0.0)
    hb = h.reshape(B, NB, BLK)
    yb = (mxq(hb, 2, "e4m3").transpose(1, 0, 2) @ mxq(f64(Wb), 2, "e4m3").transpose(0, 2, 1)).transpose(1, 0, 2)
    return np.maximum(yb.reshape(B, HID) + f64(bb), 0.0)

@@ -1,0 +1,233 @@
+from contextlib import ExitStack
+
+import concourse.mybir as mybir
+from concourse.masks import make_identity
+
+F32 = mybir.dt.float32
+BF16 = mybir.dt.bfloat16
+I32 = mybir.dt.int32
+U32 = mybir.dt.uint32
+U8 = mybir.dt.uint8
+FP8X4 = mybir.dt.float8_e4m3fn_x4
+RELU = mybir.ActivationFunctionType.Relu
+ADD = mybir.AluOpType.add
+
+P = 128
+PACK = 4
+BATCH, IN, HID, BLK = 4096, 512, 1024, 512
+CHUNKS = HID // BLK
+ROW_TILES = BATCH // P
+BLOCK_TILES = 4
+BLOCK = BLOCK_TILES * P
+BLOCKS = ROW_TILES // BLOCK_TILES
+UNITS = BLOCKS * CHUNKS
+HID_TILES = HID // P
+BANK = 512
+
+FLOPS = 2 * BATCH * IN * HID + 2 * BATCH * HID * BLK
+
+
+def tile_blockdiagmnistconvertible_pa_t_kernel(tc, x, W1_words, W1_scales, b1, Wb, bb, out):
+    nc = tc.nc
+    x_rows = x.rearrange("(p j) k -> p j k", j=ROW_TILES)
+    out_rows = out.rearrange("(p j) o -> p j o", j=ROW_TILES)
+
+    with ExitStack() as ctx:
+        keep = ctx.enter_context(tc.tile_pool(name="keep", bufs=1))
+        work = ctx.enter_context(tc.tile_pool(name="work", bufs=2))
+        results = ctx.enter_context(tc.tile_pool(name="results", bufs=4))
+        psum_t = ctx.enter_context(tc.psum_pool(name="psum_t", bufs=2))
+        psum_h = ctx.enter_context(tc.psum_pool(name="psum_h", bufs=3))
+        psum_y = ctx.enter_context(tc.psum_pool(name="psum_y", bufs=3))
+        ctx.enter_context(tc.manual_schedule())
+
+        x_sb = keep.tile([P, ROW_TILES, IN], BF16)
+        w_words = keep.tile([P, HID], U32, align_bytes=64)
+        w_scales = keep.tile([P, HID], U8, align_bytes=64)
+        wb_sb = keep.tile([P, CHUNKS * BLOCK_TILES, BLK], BF16)
+        wb_grouped = keep.tile([P, CHUNKS, BLK, PACK], BF16, align_bytes=64)
+        wb_words = keep.tile([P, CHUNKS, BLK], U32, align_bytes=64)
+        wb_scales = keep.tile([P, CHUNKS, BLK], U8, align_bytes=64)
+        b1_rows = keep.tile([P, P], BF16)
+        b1_col = keep.tile([P, HID_TILES], F32)
+        bb_bf16 = keep.tile([P, HID], BF16)
+        bb_all = keep.tile([P, HID], F32)
+        ident_f32 = keep.tile([P, P], F32)
+        ident_bf16 = keep.tile([P, P], BF16)
+
+        nc.vector.memset(w_scales[:].bitcast(I32), 0)
+        nc.vector.memset(b1_rows[:], 0.0)
+
+        def load_x(block):
+            tiles = slice(block * BLOCK_TILES, (block + 1) * BLOCK_TILES)
+            nc.sync.dma_start(out=x_sb[:, tiles, :], in_=x_rows[:, tiles, :])
+
+        load_x(0)
+        for quadrant in range(4):
+            nc.sync.dma_start(
+                out=w_scales[32 * quadrant : 32 * quadrant + 4, :].bitcast(I32),
+                in_=W1_scales[0, 4 * quadrant : 4 * quadrant + 4, :].bitcast(I32),
+            )
+        nc.sync.dma_start(
+            out=w_words[:].bitcast(I32),
+            in_=W1_words[0].rearrange("p n t -> p (n t)").bitcast(I32),
+        )
+        load_x(1)
+        nc.sync.dma_start(out=wb_sb[:], in_=Wb.rearrange("n (a p) k -> p (n a) k", p=P))
+        for block in range(2, BLOCKS):
+            load_x(block)
+        nc.scalar.dma_start(out=b1_rows[0:HID_TILES, :], in_=b1.rearrange("(m p) -> m p", p=P))
+        nc.scalar.dma_start(out=bb_bf16[:], in_=bb.partition_broadcast(P))
+
+        make_identity(nc, ident_bf16[:])
+        make_identity(nc, ident_f32[:])
+
+        b1_t = psum_t.tile([P, P], BF16, tag="t")
+        nc.tensor.transpose(b1_t[:], b1_rows[:], ident_bf16[:])
+        nc.vector.tensor_copy(out=b1_col[:], in_=b1_t[:, 0:HID_TILES])
+
+        x_grouped = {}
+        x_codes = {}
+        h_planes = {}
+        h_grouped = {}
+        h_codes = {}
+        out_tiles = {}
+
+        def transpose_x(block):
+            xg = work.tile([P, BLOCK * PACK], BF16, align_bytes=64)
+            xg_words = xg[:].bitcast(F32).rearrange("p (c u) -> p c u", u=2)
+            for half in range(2):
+                xt = psum_t.tile([P, 2, BANK // 2], F32, tag="t")
+                for pair in range(2):
+                    words = x_sb[:, block * BLOCK_TILES + 2 * half + pair, :].bitcast(F32)
+                    for u in range(2):
+                        nc.tensor.transpose(
+                            xt[:, u, pair * P : (pair + 1) * P], words[:, u : IN // 2 : 2], ident_f32[:]
+                        )
+                nc.scalar.copy(
+                    out=xg_words[:, half * (BANK // 2) : (half + 1) * (BANK // 2), :],
+                    in_=xt[:].rearrange("p u c -> p c u"),
+                )
+            x_grouped[block] = xg
+
+        def quantise_x(block):
+            xq = work.tile([P, BLOCK], U32, align_bytes=64)
+            xs = work.tile([P, BLOCK], U8, align_bytes=64)
+            nc.vector.quantize_mx(out=xq[:].bitcast(FP8X4), scales=xs[:], in_=x_grouped[block][:])
+            x_codes[block] = (xq, xs)
+
+        def transpose_wb(n):
+            for half in range(2):
+                wt = psum_t.tile([P, 2, PACK, P], BF16, tag="t")
+                for a in range(2):
+                    for t in range(PACK):
+                        nc.tensor.transpose(
+                            wt[:, a, t, :],
+                            wb_sb[:, n * BLOCK_TILES + 2 * half + a, t * P : (t + 1) * P],
+                            ident_bf16[:],
+                        )
+                dst = wb_grouped[:, n, 2 * half * P : 2 * (half + 1) * P, :].rearrange("p (a o) t -> p a o t", a=2)
+                src = wt[:].rearrange("p a t o -> p a o t")
+                if half == 0:
+                    nc.vector.tensor_copy(out=dst, in_=src)
+                else:
+                    nc.scalar.copy(out=dst, in_=src)
+
+        def quantise_wb(n):
+            nc.vector.quantize_mx(
+                out=wb_words[:, n, :].bitcast(FP8X4),
+                scales=wb_scales[:, n, :],
+                in_=wb_grouped[:, n, :, :].rearrange("p o t -> p (o t)"),
+            )
+
+        def first_matmul(unit, t):
+            block, n = divmod(unit, CHUNKS)
+            if t == 0:
+                planes = work.tile([P, PACK, BLOCK], BF16, bufs=3)
+                h_planes[unit] = planes
+            m = n * PACK + t
+            xq, xs = x_codes[block]
+            acc = psum_h.tile([P, BANK], F32)
+            nc.tensor.matmul_mx(
+                out=acc[:],
+                lhsT=w_words[:, m * P : (m + 1) * P].bitcast(FP8X4),
+                lhsT_scale=w_scales[:, m * P : (m + 1) * P],
+                rhs=xq[:].bitcast(FP8X4),
+                rhs_scale=xs[:],
+                start=True,
+                stop=True,
+            )
+            nc.scalar.activation(out=h_planes[unit][:, t, :], in_=acc[:], func=RELU, bias=b1_col[:, m : m + 1], scale=1.0)
+
+        def group_h(unit):
+            hg = work.tile([P, BLOCK, PACK], BF16, align_bytes=64)
+            nc.vector.tensor_copy(
+                out=hg[:].rearrange("p (c i) t -> p c t i", i=4),
+                in_=h_planes[unit][:].rearrange("p t (c i) -> p c t i", i=4),
+            )
+            h_grouped[unit] = hg
+
+        def quantise_h(unit):
+            hq = work.tile([P, BLOCK], U32, align_bytes=64)
+            hs = work.tile([P, BLOCK], U8, align_bytes=64)
+            nc.vector.quantize_mx(
+                out=hq[:].bitcast(FP8X4), scales=hs[:], in_=h_grouped[unit][:].rearrange("p c t -> p (c t)")
+            )
+            h_codes[unit] = (hq, hs)
+
+        def second_matmul(unit, j):
+            n = unit % CHUNKS
+            if j == 0:
+                res = results.tile([P, BLOCK_TILES, BLK], F32)
+                out_tiles[unit] = res
+            hq, hs = h_codes[unit]
+            acc = psum_y.tile([P, BANK], F32)
+            nc.tensor.matmul_mx(
+                out=acc[:],
+                lhsT=hq[:, j * P : (j + 1) * P].bitcast(FP8X4),
+                lhsT_scale=hs[:, j * P : (j + 1) * P],
+                rhs=wb_words[:, n, :].bitcast(FP8X4),
+                rhs_scale=wb_scales[:, n, :],
+                start=True,
+                stop=True,
+            )
+            nc.vector.tensor_tensor(out=out_tiles[unit][:, j, :], in0=acc[:], in1=bb_all[:, n * BLK : (n + 1) * BLK], op=ADD)
+
+        def relu_and_store(unit, j):
+            block, n = divmod(unit, CHUNKS)
+            res = out_tiles[unit]
+            if j == BLOCK_TILES - 1:
+                nc.vector.tensor_scalar_max(out=res[:, j, :], in0=res[:, j, :], scalar1=0.0)
+            else:
+                nc.scalar.activation(out=res[:, j, :], in_=res[:, j, :], func=RELU)
+            if j % 2 == 1:
+                nc.sync.dma_start(
+                    out=out_rows[:, block * BLOCK_TILES + j - 1 : block * BLOCK_TILES + j + 1, n * BLK : (n + 1) * BLK],
+                    in_=res[:, j - 1 : j + 1, :],
+                )
+
+        transpose_x(0)
+        quantise_x(0)
+        nc.vector.tensor_copy(out=bb_all[:], in_=bb_bf16[:])
+        for step in range(UNITS + 3):
+            next_block = step // CHUNKS + 1
+            new_block = step % CHUNKS == 0 and next_block < BLOCKS
+            if new_block:
+                transpose_x(next_block)
+            if 0 <= step - 1 < UNITS:
+                group_h(step - 1)
+            if 0 <= step - 1 < CHUNKS:
+                transpose_wb(step - 1)
+            for i in range(PACK):
+                if step < UNITS:
+                    first_matmul(step, i)
+                if 0 <= step - 2 < UNITS:
+                    second_matmul(step - 2, i)
+                if 0 <= step - 3 < UNITS:
+                    relu_and_store(step - 3, i)
+            if 0 <= step - 1 < UNITS:
+                quantise_h(step - 1)
+            if 0 <= step - 1 < CHUNKS:
+                quantise_wb(step - 1)
+            if new_block:
+                quantise_x(next_block)

@@ -11,6 +11,7 @@ U8 = mybir.dt.uint8
 FP8X4 = mybir.dt.float8_e4m3fn_x4
 RELU = mybir.ActivationFunctionType.Relu
 ADD = mybir.AluOpType.add
+MAX = mybir.AluOpType.max
 
 P = 128
 PACK = 4
@@ -161,9 +162,14 @@ def tile_blockdiagmnistconvertible_pa_t_kernel(tc, x, W1_words, W1_scales, b1, W
 
         def group_h(unit):
             hg = work.tile([P, BLOCK, PACK], BF16, align_bytes=64)
+            half = BLOCK // 2
             nc.vector.tensor_copy(
-                out=hg[:].rearrange("p (c i) t -> p c t i", i=4),
-                in_=h_planes[unit][:].rearrange("p t (c i) -> p c t i", i=4),
+                out=hg[:, 0:half, :].rearrange("p (c i) t -> p c t i", i=4),
+                in_=h_planes[unit][:, :, 0:half].rearrange("p t (c i) -> p c t i", i=4),
+            )
+            nc.scalar.copy(
+                out=hg[:, half:BLOCK, :].rearrange("p (c i) t -> p c t i", i=4),
+                in_=h_planes[unit][:, :, half:BLOCK].rearrange("p t (c i) -> p c t i", i=4),
             )
             h_grouped[unit] = hg
 
@@ -197,9 +203,9 @@ def tile_blockdiagmnistconvertible_pa_t_kernel(tc, x, W1_words, W1_scales, b1, W
             block, n = divmod(unit, CHUNKS)
             res = out_tiles[unit]
             if j == BLOCK_TILES - 1:
-                nc.vector.tensor_scalar_max(out=res[:, j, :], in0=res[:, j, :], scalar1=0.0)
-            else:
                 nc.scalar.activation(out=res[:, j, :], in_=res[:, j, :], func=RELU)
+            else:
+                nc.gpsimd.tensor_scalar(out=res[:, j, :], in0=res[:, j, :], scalar1=0.0, scalar2=0.0, op0=MAX, op1=ADD)
             if j % 2 == 1:
                 nc.sync.dma_start(
                     out=out_rows[:, block * BLOCK_TILES + j - 1 : block * BLOCK_TILES + j + 1, n * BLK : (n + 1) * BLK],
@@ -219,10 +225,10 @@ def tile_blockdiagmnistconvertible_pa_t_kernel(tc, x, W1_words, W1_scales, b1, W
             if 0 <= step - 1 < CHUNKS:
                 transpose_wb(step - 1)
             for i in range(PACK):
-                if step < UNITS:
-                    first_matmul(step, i)
                 if 0 <= step - 2 < UNITS:
                     second_matmul(step - 2, i)
+                if step < UNITS:
+                    first_matmul(step, i)
                 if 0 <= step - 3 < UNITS:
                     relu_and_store(step - 3, i)
             if 0 <= step - 1 < UNITS:

@@ -11,7 +11,7 @@ U8 = mybir.dt.uint8
 FP8X4 = mybir.dt.float8_e4m3fn_x4
 RELU = mybir.ActivationFunctionType.Relu
 ADD = mybir.AluOpType.add
-MAX = mybir.AluOpType.max
+MULT = mybir.AluOpType.mult
 
 P = 128
 PACK = 4
@@ -161,15 +161,9 @@ def tile_blockdiagmnistconvertible_pa_t_kernel(tc, x, W1_words, W1_scales, b1, W
             nc.scalar.activation(out=h_planes[unit][:, t, :], in_=acc[:], func=RELU, bias=b1_col[:, m : m + 1], scale=1.0)
 
         def group_h(unit):
-            hg = work.tile([P, BLOCK, PACK], BF16, align_bytes=64)
-            half = BLOCK // 2
-            nc.vector.tensor_copy(
-                out=hg[:, 0:half, :].rearrange("p (c i) t -> p c t i", i=4),
-                in_=h_planes[unit][:, :, 0:half].rearrange("p t (c i) -> p c t i", i=4),
-            )
-            nc.scalar.copy(
-                out=hg[:, half:BLOCK, :].rearrange("p (c i) t -> p c t i", i=4),
-                in_=h_planes[unit][:, :, half:BLOCK].rearrange("p t (c i) -> p c t i", i=4),
+            hg = work.tile([P, BLOCK, PACK], BF16, align_bytes=64, bufs=1)
+            nc.gpsimd.tensor_scalar(
+                out=hg[:], in0=h_planes[unit][:].rearrange("p t c -> p c t"), scalar1=1.0, scalar2=0.0, op0=MULT, op1=ADD
             )
             h_grouped[unit] = hg
 
@@ -199,18 +193,15 @@ def tile_blockdiagmnistconvertible_pa_t_kernel(tc, x, W1_words, W1_scales, b1, W
             )
             nc.vector.tensor_tensor(out=out_tiles[unit][:, j, :], in0=acc[:], in1=bb_all[:, n * BLK : (n + 1) * BLK], op=ADD)
 
-        def relu_and_store(unit, j):
+        def relu_and_store(unit, pair):
             block, n = divmod(unit, CHUNKS)
-            res = out_tiles[unit]
-            if j == BLOCK_TILES - 1:
-                nc.scalar.activation(out=res[:, j, :], in_=res[:, j, :], func=RELU)
+            res = out_tiles[unit][:, 2 * pair : 2 * pair + 2, :]
+            if pair == 0:
+                nc.scalar.activation(out=res, in_=res, func=RELU)
             else:
-                nc.gpsimd.tensor_scalar(out=res[:, j, :], in0=res[:, j, :], scalar1=0.0, scalar2=0.0, op0=MAX, op1=ADD)
-            if j % 2 == 1:
-                nc.sync.dma_start(
-                    out=out_rows[:, block * BLOCK_TILES + j - 1 : block * BLOCK_TILES + j + 1, n * BLK : (n + 1) * BLK],
-                    in_=res[:, j - 1 : j + 1, :],
-                )
+                nc.vector.tensor_scalar_max(out=res, in0=res, scalar1=0.0)
+            first_tile = block * BLOCK_TILES + 2 * pair
+            nc.sync.dma_start(out=out_rows[:, first_tile : first_tile + 2, n * BLK : (n + 1) * BLK], in_=res)
 
         transpose_x(0)
         quantise_x(0)
@@ -229,11 +220,12 @@ def tile_blockdiagmnistconvertible_pa_t_kernel(tc, x, W1_words, W1_scales, b1, W
                     second_matmul(step - 2, i)
                 if step < UNITS:
                     first_matmul(step, i)
-                if 0 <= step - 3 < UNITS:
-                    relu_and_store(step - 3, i)
             if 0 <= step - 1 < UNITS:
                 quantise_h(step - 1)
             if 0 <= step - 1 < CHUNKS:
                 quantise_wb(step - 1)
             if new_block:
                 quantise_x(next_block)
+            if 0 <= step - 3 < UNITS:
+                relu_and_store(step - 3, 0)
+                relu_and_store(step - 3, 1)

@@ -22,6 +22,9 @@ BLOCK_TILES = 4
 BLOCK = BLOCK_TILES * P
 BLOCKS = ROW_TILES // BLOCK_TILES
 UNITS = BLOCKS * CHUNKS
+HALF = BLOCK // 2
+HALVES = 2 * BLOCKS
+X_LEAD = 2
 HID_TILES = HID // P
 BANK = 512
 
@@ -59,11 +62,17 @@ def tile_blockdiagmnistconvertible_pa_t_kernel(tc, x, W1_words, W1_scales, b1, W
         nc.vector.memset(w_scales[:].bitcast(I32), 0)
         nc.vector.memset(b1_rows[:], 0.0)
 
-        def load_x(block):
-            tiles = slice(block * BLOCK_TILES, (block + 1) * BLOCK_TILES)
+        def load_x(half):
+            tiles = slice(2 * half, 2 * half + 2)
             nc.sync.dma_start(out=x_sb[:, tiles, :], in_=x_rows[:, tiles, :])
 
+        def load_wb(n):
+            nc.sync.dma_start(
+                out=wb_sb[:, n * BLOCK_TILES : (n + 1) * BLOCK_TILES, :], in_=Wb[n].rearrange("(a p) k -> p a k", p=P)
+            )
+
         load_x(0)
+        load_x(1)
         for quadrant in range(4):
             nc.sync.dma_start(
                 out=w_scales[32 * quadrant : 32 * quadrant + 4, :].bitcast(I32),
@@ -73,10 +82,13 @@ def tile_blockdiagmnistconvertible_pa_t_kernel(tc, x, W1_words, W1_scales, b1, W
             out=w_words[:].bitcast(I32),
             in_=W1_words[0].rearrange("p n t -> p (n t)").bitcast(I32),
         )
-        load_x(1)
-        nc.sync.dma_start(out=wb_sb[:], in_=Wb.rearrange("n (a p) k -> p (n a) k", p=P))
-        for block in range(2, BLOCKS):
-            load_x(block)
+        load_x(2)
+        load_wb(0)
+        load_x(3)
+        load_x(4)
+        load_wb(1)
+        for half in range(5, HALVES):
+            load_x(half)
         nc.scalar.dma_start(out=b1_rows[0:HID_TILES, :], in_=b1.rearrange("(m p) -> m p", p=P))
         nc.scalar.dma_start(out=bb_bf16[:], in_=bb.partition_broadcast(P))
 
@@ -87,49 +99,54 @@ def tile_blockdiagmnistconvertible_pa_t_kernel(tc, x, W1_words, W1_scales, b1, W
         nc.tensor.transpose(b1_t[:], b1_rows[:], ident_bf16[:])
         nc.vector.tensor_copy(out=b1_col[:], in_=b1_t[:, 0:HID_TILES])
 
+        x_banks = {}
         x_grouped = {}
         x_codes = {}
+        h_banks = {}
         h_planes = {}
         h_grouped = {}
         h_codes = {}
         out_tiles = {}
 
-        def transpose_x(block):
-            xg = work.tile([P, BLOCK * PACK], BF16, align_bytes=64)
-            xg_words = xg[:].bitcast(F32).rearrange("p (c u) -> p c u", u=2)
-            for half in range(2):
-                xt = psum_t.tile([P, 2, BANK // 2], F32, tag="t")
-                for pair in range(2):
-                    words = x_sb[:, block * BLOCK_TILES + 2 * half + pair, :].bitcast(F32)
-                    for u in range(2):
-                        nc.tensor.transpose(
-                            xt[:, u, pair * P : (pair + 1) * P], words[:, u : IN // 2 : 2], ident_f32[:]
-                        )
-                nc.scalar.copy(
-                    out=xg_words[:, half * (BANK // 2) : (half + 1) * (BANK // 2), :],
-                    in_=xt[:].rearrange("p u c -> p c u"),
-                )
-            x_grouped[block] = xg
+        def transpose_x(half):
+            xt = psum_t.tile([P, 2, HALF], F32, tag="t")
+            for pair in range(2):
+                words = x_sb[:, 2 * half + pair, :].bitcast(F32)
+                for u in range(2):
+                    nc.tensor.transpose(xt[:, u, pair * P : (pair + 1) * P], words[:, u : IN // 2 : 2], ident_f32[:])
+            x_banks[half] = xt
 
-        def quantise_x(block):
-            xq = work.tile([P, BLOCK], U32, align_bytes=64)
-            xs = work.tile([P, BLOCK], U8, align_bytes=64)
-            nc.vector.quantize_mx(out=xq[:].bitcast(FP8X4), scales=xs[:], in_=x_grouped[block][:])
-            x_codes[block] = (xq, xs)
+        def group_x(half):
+            xg = work.tile([P, HALF * PACK], BF16, align_bytes=64)
+            nc.vector.tensor_copy(
+                out=xg[:].bitcast(F32).rearrange("p (c u) -> p c u", u=2),
+                in_=x_banks[half][:].rearrange("p u c -> p c u"),
+            )
+            x_grouped[half] = xg
+
+        def quantise_x(half):
+            block, side = divmod(half, 2)
+            if side == 0:
+                xq = work.tile([P, BLOCK], U32, align_bytes=64, bufs=3)
+                xs = work.tile([P, BLOCK], U8, align_bytes=64, bufs=3)
+                x_codes[block] = (xq, xs)
+            xq, xs = x_codes[block]
+            cols = slice(side * HALF, (side + 1) * HALF)
+            nc.vector.quantize_mx(out=xq[:, cols].bitcast(FP8X4), scales=xs[:, cols], in_=x_grouped[half][:])
 
         def transpose_wb(n):
-            for half in range(2):
+            for side in range(2):
                 wt = psum_t.tile([P, 2, PACK, P], BF16, tag="t")
                 for a in range(2):
                     for t in range(PACK):
                         nc.tensor.transpose(
                             wt[:, a, t, :],
-                            wb_sb[:, n * BLOCK_TILES + 2 * half + a, t * P : (t + 1) * P],
+                            wb_sb[:, n * BLOCK_TILES + 2 * side + a, t * P : (t + 1) * P],
                             ident_bf16[:],
                         )
-                dst = wb_grouped[:, n, 2 * half * P : 2 * (half + 1) * P, :].rearrange("p (a o) t -> p a o t", a=2)
+                dst = wb_grouped[:, n, 2 * side * P : 2 * (side + 1) * P, :].rearrange("p (a o) t -> p a o t", a=2)
                 src = wt[:].rearrange("p a t o -> p a o t")
-                if half == 0:
+                if side == 0:
                     nc.vector.tensor_copy(out=dst, in_=src)
                 else:
                     nc.scalar.copy(out=dst, in_=src)
@@ -143,9 +160,6 @@ def tile_blockdiagmnistconvertible_pa_t_kernel(tc, x, W1_words, W1_scales, b1, W
 
         def first_matmul(unit, t):
             block, n = divmod(unit, CHUNKS)
-            if t == 0:
-                planes = work.tile([P, PACK, BLOCK], BF16, bufs=3)
-                h_planes[unit] = planes
             m = n * PACK + t
             xq, xs = x_codes[block]
             acc = psum_h.tile([P, BANK], F32)
@@ -158,6 +172,14 @@ def tile_blockdiagmnistconvertible_pa_t_kernel(tc, x, W1_words, W1_scales, b1, W
                 start=True,
                 stop=True,
             )
+            h_banks[(unit, t)] = acc
+
+        def leave_h(unit, t):
+            if t == 0:
+                planes = work.tile([P, PACK, BLOCK], BF16, bufs=3)
+                h_planes[unit] = planes
+            m = (unit % CHUNKS) * PACK + t
+            acc = h_banks[(unit, t)]
             nc.scalar.activation(out=h_planes[unit][:, t, :], in_=acc[:], func=RELU, bias=b1_col[:, m : m + 1], scale=1.0)
 
         def group_h(unit):
@@ -193,26 +215,28 @@ def tile_blockdiagmnistconvertible_pa_t_kernel(tc, x, W1_words, W1_scales, b1, W
             )
             nc.vector.tensor_tensor(out=out_tiles[unit][:, j, :], in0=acc[:], in1=bb_all[:, n * BLK : (n + 1) * BLK], op=ADD)
 
-        def relu_and_store(unit, pair):
+        def relu_and_store(unit):
             block, n = divmod(unit, CHUNKS)
-            res = out_tiles[unit][:, 2 * pair : 2 * pair + 2, :]
-            if pair == 0:
-                nc.scalar.activation(out=res, in_=res, func=RELU)
-            else:
-                nc.vector.tensor_scalar_max(out=res, in0=res, scalar1=0.0)
-            first_tile = block * BLOCK_TILES + 2 * pair
-            nc.sync.dma_start(out=out_rows[:, first_tile : first_tile + 2, n * BLK : (n + 1) * BLK], in_=res)
+            res = out_tiles[unit]
+            nc.vector.tensor_scalar_max(out=res[:, 3, :], in0=res[:, 3, :], scalar1=0.0)
+            nc.scalar.activation(out=res[:, 0:2, :], in_=res[:, 0:2, :], func=RELU)
+            nc.scalar.activation(out=res[:, 2, :], in_=res[:, 2, :], func=RELU)
+            for first in (0, 2):
+                tiles = slice(block * BLOCK_TILES + first, block * BLOCK_TILES + first + 2)
+                nc.sync.dma_start(out=out_rows[:, tiles, n * BLK : (n + 1) * BLK], in_=res[:, first : first + 2, :])
 
-        transpose_x(0)
-        quantise_x(0)
+        for half in range(X_LEAD):
+            transpose_x(half)
+            group_x(half)
+            quantise_x(half)
+        transpose_x(X_LEAD)
         nc.vector.tensor_copy(out=bb_all[:], in_=bb_bf16[:])
         for step in range(UNITS + 3):
-            next_block = step // CHUNKS + 1
-            new_block = step % CHUNKS == 0 and next_block < BLOCKS
-            if new_block:
-                transpose_x(next_block)
+            half = step + X_LEAD
             if 0 <= step - 1 < UNITS:
                 group_h(step - 1)
+            if half < HALVES:
+                group_x(half)
             if 0 <= step - 1 < CHUNKS:
                 transpose_wb(step - 1)
             for i in range(PACK):
@@ -220,12 +244,14 @@ def tile_blockdiagmnistconvertible_pa_t_kernel(tc, x, W1_words, W1_scales, b1, W
                     second_matmul(step - 2, i)
                 if step < UNITS:
                     first_matmul(step, i)
+                    leave_h(step, i)
+            if half + 1 < HALVES:
+                transpose_x(half + 1)
             if 0 <= step - 1 < UNITS:
                 quantise_h(step - 1)
             if 0 <= step - 1 < CHUNKS:
                 quantise_wb(step - 1)
-            if new_block:
-                quantise_x(next_block)
+            if half < HALVES:
+                quantise_x(half)
             if 0 <= step - 3 < UNITS:
-                relu_and_store(step - 3, 0)
-                relu_and_store(step - 3, 1)
+                relu_and_store(step - 3)

@@ -12,6 +12,7 @@ FP8X4 = mybir.dt.float8_e4m3fn_x4
 RELU = mybir.ActivationFunctionType.Relu
 ADD = mybir.AluOpType.add
 MULT = mybir.AluOpType.mult
+MAX = mybir.AluOpType.max
 
 P = 128
 PACK = 4
@@ -59,6 +60,10 @@ def tile_blockdiagmnistconvertible_pa_t_kernel(tc, x, W1_words, W1_scales, b1, W
         ident_f32 = keep.tile([P, P], F32)
         ident_bf16 = keep.tile([P, P], BF16)
 
+        zeros = keep.tile([P, BANK], BF16)
+        nc.vector.memset(zeros[:], 0.0)
+        warm = keep.tile([P, 1], F32)
+        nc.vector.memset(warm[:], 0.0)
         nc.vector.memset(w_scales[:].bitcast(I32), 0)
         nc.vector.memset(b1_rows[:], 0.0)
 
@@ -71,6 +76,13 @@ def tile_blockdiagmnistconvertible_pa_t_kernel(tc, x, W1_words, W1_scales, b1, W
                 out=wb_sb[:, n * BLOCK_TILES : (n + 1) * BLOCK_TILES, :], in_=Wb[n].rearrange("(a p) k -> p a k", p=P)
             )
 
+        def load_w(n):
+            cols = slice(n * BLK, (n + 1) * BLK)
+            nc.sync.dma_start(
+                out=w_words[:, cols].bitcast(I32),
+                in_=W1_words[0].rearrange("p n t -> p (n t)")[:, n * BLK * PACK : (n + 1) * BLK * PACK].bitcast(I32),
+            )
+
         load_x(0)
         load_x(1)
         for quadrant in range(4):
@@ -78,78 +90,92 @@ def tile_blockdiagmnistconvertible_pa_t_kernel(tc, x, W1_words, W1_scales, b1, W
                 out=w_scales[32 * quadrant : 32 * quadrant + 4, :].bitcast(I32),
                 in_=W1_scales[0, 4 * quadrant : 4 * quadrant + 4, :].bitcast(I32),
             )
-        nc.sync.dma_start(
-            out=w_words[:].bitcast(I32),
-            in_=W1_words[0].rearrange("p n t -> p (n t)").bitcast(I32),
-        )
+        load_w(0)
         load_x(2)
-        load_wb(0)
         load_x(3)
+        load_wb(0)
+        load_w(1)
         load_x(4)
+        nc.sync.dma_start(out=bb_bf16[:], in_=bb.partition_broadcast(P))
         load_wb(1)
         for half in range(5, HALVES):
             load_x(half)
         nc.scalar.dma_start(out=b1_rows[0:HID_TILES, :], in_=b1.rearrange("(m p) -> m p", p=P))
-        nc.scalar.dma_start(out=bb_bf16[:], in_=bb.partition_broadcast(P))
 
-        make_identity(nc, ident_bf16[:])
         make_identity(nc, ident_f32[:])
+        make_identity(nc, ident_bf16[:])
+        nc.scalar.activation(out=warm[:], in_=warm[:], func=RELU)
 
-        b1_t = psum_t.tile([P, P], BF16, tag="t")
-        nc.tensor.transpose(b1_t[:], b1_rows[:], ident_bf16[:])
-        nc.vector.tensor_copy(out=b1_col[:], in_=b1_t[:, 0:HID_TILES])
 
         x_banks = {}
         x_grouped = {}
         x_codes = {}
-        h_banks = {}
+        wb_banks = {}
         h_planes = {}
         h_grouped = {}
         h_codes = {}
         out_tiles = {}
+        WHOLE = (0, BLOCK)
+        SIDES = ((0, HALF), (HALF, BLOCK))
 
-        def transpose_x(half):
-            xt = psum_t.tile([P, 2, HALF], F32, tag="t")
+        def spread_b1():
+            b1_t = psum_t.tile([P, P], BF16, tag="t")
+            nc.tensor.transpose(b1_t[:], b1_rows[:], ident_bf16[:])
+            nc.vector.tensor_copy(out=b1_col[:], in_=b1_t[:, 0:HID_TILES])
+
+        def warm_up(count):
+            for i in range(count):
+                idle = psum_t.tile([P, BANK], F32, tag="t")
+                nc.tensor.matmul(idle[:], lhsT=zeros[:, 0:P], rhs=zeros[:], start=True, stop=True)
+
+        def transpose_x(half, early=False):
+            pool, tag = (psum_y, "y") if early else (psum_t, "t")
+            xt = pool.tile([P, 2, HALF], F32, tag=tag)
             for pair in range(2):
                 words = x_sb[:, 2 * half + pair, :].bitcast(F32)
                 for u in range(2):
                     nc.tensor.transpose(xt[:, u, pair * P : (pair + 1) * P], words[:, u : IN // 2 : 2], ident_f32[:])
             x_banks[half] = xt
 
-        def group_x(half):
-            xg = work.tile([P, HALF * PACK], BF16, align_bytes=64)
-            nc.vector.tensor_copy(
-                out=xg[:].bitcast(F32).rearrange("p (c u) -> p c u", u=2),
-                in_=x_banks[half][:].rearrange("p u c -> p c u"),
-            )
-            x_grouped[half] = xg
-
-        def quantise_x(half):
+        def group_x(half, engine):
             block, side = divmod(half, 2)
             if side == 0:
+                xg = work.tile([P, BLOCK * PACK], BF16, align_bytes=64, bufs=2)
+                x_grouped[block] = xg
+            xg = x_grouped[block][:, side * HALF * PACK : (side + 1) * HALF * PACK]
+            copy = nc.vector.tensor_copy if engine == "V" else nc.scalar.copy
+            copy(
+                out=xg.bitcast(F32).rearrange("p (c u) -> p c u", u=2),
+                in_=x_banks[half][:].rearrange("p u c -> p c u"),
+            )
+
+        def quantise_x(block, span):
+            if block not in x_codes:
                 xq = work.tile([P, BLOCK], U32, align_bytes=64, bufs=3)
                 xs = work.tile([P, BLOCK], U8, align_bytes=64, bufs=3)
                 x_codes[block] = (xq, xs)
             xq, xs = x_codes[block]
-            cols = slice(side * HALF, (side + 1) * HALF)
-            nc.vector.quantize_mx(out=xq[:, cols].bitcast(FP8X4), scales=xs[:, cols], in_=x_grouped[half][:])
+            first, last = span
+            nc.vector.quantize_mx(
+                out=xq[:, first:last].bitcast(FP8X4), scales=xs[:, first:last], in_=x_grouped[block][:, first * PACK : last * PACK]
+            )
 
-        def transpose_wb(n):
-            for side in range(2):
-                wt = psum_t.tile([P, 2, PACK, P], BF16, tag="t")
-                for a in range(2):
-                    for t in range(PACK):
-                        nc.tensor.transpose(
-                            wt[:, a, t, :],
-                            wb_sb[:, n * BLOCK_TILES + 2 * side + a, t * P : (t + 1) * P],
-                            ident_bf16[:],
-                        )
-                dst = wb_grouped[:, n, 2 * side * P : 2 * (side + 1) * P, :].rearrange("p (a o) t -> p a o t", a=2)
-                src = wt[:].rearrange("p a t o -> p a o t")
-                if side == 0:
-                    nc.vector.tensor_copy(out=dst, in_=src)
-                else:
-                    nc.scalar.copy(out=dst, in_=src)
+        def transpose_wb(n, side, early=False):
+            pool, tag = (psum_y, "y") if early else (psum_t, "t")
+            wt = pool.tile([P, 2, PACK, P], BF16, tag=tag)
+            for a in range(2):
+                for t in range(PACK):
+                    nc.tensor.transpose(
+                        wt[:, a, t, :],
+                        wb_sb[:, n * BLOCK_TILES + 2 * side + a, t * P : (t + 1) * P],
+                        ident_bf16[:],
+                    )
+            wb_banks[(n, side)] = wt
+
+        def leave_wb(n, side, engine):
+            dst = wb_grouped[:, n, 2 * side * P : 2 * (side + 1) * P, :].rearrange("p (a o) t -> p a o t", a=2)
+            copy = nc.vector.tensor_copy if engine == "V" else nc.scalar.copy
+            copy(out=dst, in_=wb_banks[(n, side)][:].rearrange("p a t o -> p a o t"))
 
         def quantise_wb(n):
             nc.vector.quantize_mx(
@@ -158,52 +184,62 @@ def tile_blockdiagmnistconvertible_pa_t_kernel(tc, x, W1_words, W1_scales, b1, W
                 in_=wb_grouped[:, n, :, :].rearrange("p o t -> p (o t)"),
             )
 
-        def first_matmul(unit, t):
+        def hidden(unit, t, span):
             block, n = divmod(unit, CHUNKS)
             m = n * PACK + t
             xq, xs = x_codes[block]
+            first, last = span
             acc = psum_h.tile([P, BANK], F32)
             nc.tensor.matmul_mx(
-                out=acc[:],
+                out=acc[:, 0 : last - first],
                 lhsT=w_words[:, m * P : (m + 1) * P].bitcast(FP8X4),
                 lhsT_scale=w_scales[:, m * P : (m + 1) * P],
-                rhs=xq[:].bitcast(FP8X4),
-                rhs_scale=xs[:],
+                rhs=xq[:, first:last].bitcast(FP8X4),
+                rhs_scale=xs[:, first:last],
                 start=True,
                 stop=True,
             )
-            h_banks[(unit, t)] = acc
-
-        def leave_h(unit, t):
-            if t == 0:
+            if unit not in h_planes:
                 planes = work.tile([P, PACK, BLOCK], BF16, bufs=3)
                 h_planes[unit] = planes
-            m = (unit % CHUNKS) * PACK + t
-            acc = h_banks[(unit, t)]
-            nc.scalar.activation(out=h_planes[unit][:, t, :], in_=acc[:], func=RELU, bias=b1_col[:, m : m + 1], scale=1.0)
-
-        def group_h(unit):
-            hg = work.tile([P, BLOCK, PACK], BF16, align_bytes=64, bufs=1)
-            nc.gpsimd.tensor_scalar(
-                out=hg[:], in0=h_planes[unit][:].rearrange("p t c -> p c t"), scalar1=1.0, scalar2=0.0, op0=MULT, op1=ADD
+            nc.scalar.activation(
+                out=h_planes[unit][:, t, first:last], in_=acc[:, 0 : last - first], func=RELU, bias=b1_col[:, m : m + 1], scale=1.0
             )
-            h_grouped[unit] = hg
 
-        def quantise_h(unit):
-            hq = work.tile([P, BLOCK], U32, align_bytes=64)
-            hs = work.tile([P, BLOCK], U8, align_bytes=64)
+        def group_h(unit, span, engine):
+            if unit not in h_grouped:
+                hg = work.tile([P, BLOCK, PACK], BF16, align_bytes=64, bufs=1)
+                h_grouped[unit] = hg
+            first, last = span
+            dst = h_grouped[unit][:, first:last, :].rearrange("p (c i) t -> p c t i", i=4)
+            src = h_planes[unit][:, :, first:last].rearrange("p t (c i) -> p c t i", i=4)
+            if engine == "G":
+                nc.gpsimd.tensor_scalar(out=dst, in0=src, scalar1=1.0, scalar2=0.0, op0=MULT, op1=ADD)
+            elif engine == "V":
+                nc.vector.tensor_copy(out=dst, in_=src)
+            else:
+                nc.scalar.copy(out=dst, in_=src)
+
+        def quantise_h(unit, span):
+            if unit not in h_codes:
+                hq = work.tile([P, BLOCK], U32, align_bytes=64, bufs=2)
+                hs = work.tile([P, BLOCK], U8, align_bytes=64, bufs=2)
+                h_codes[unit] = (hq, hs)
+            hq, hs = h_codes[unit]
+            first, last = span
             nc.vector.quantize_mx(
-                out=hq[:].bitcast(FP8X4), scales=hs[:], in_=h_grouped[unit][:].rearrange("p c t -> p (c t)")
+                out=hq[:, first:last].bitcast(FP8X4),
+                scales=hs[:, first:last],
+                in_=h_grouped[unit][:, first:last, :].rearrange("p c t -> p (c t)"),
             )
-            h_codes[unit] = (hq, hs)
 
         def second_matmul(unit, j):
             n = unit % CHUNKS
-            if j == 0:
+            if unit not in out_tiles:
                 res = results.tile([P, BLOCK_TILES, BLK], F32)
                 out_tiles[unit] = res
             hq, hs = h_codes[unit]
-            acc = psum_y.tile([P, BANK], F32)
+            acc = psum_y.tile([P, BANK], F32, tag="y")
             nc.tensor.matmul_mx(
                 out=acc[:],
                 lhsT=hq[:, j * P : (j + 1) * P].bitcast(FP8X4),
@@ -215,43 +251,95 @@ def tile_blockdiagmnistconvertible_pa_t_kernel(tc, x, W1_words, W1_scales, b1, W
             )
             nc.vector.tensor_tensor(out=out_tiles[unit][:, j, :], in0=acc[:], in1=bb_all[:, n * BLK : (n + 1) * BLK], op=ADD)
 
-        def relu_and_store(unit):
-            block, n = divmod(unit, CHUNKS)
-            res = out_tiles[unit]
-            nc.vector.tensor_scalar_max(out=res[:, 3, :], in0=res[:, 3, :], scalar1=0.0)
-            nc.scalar.activation(out=res[:, 0:2, :], in_=res[:, 0:2, :], func=RELU)
-            nc.scalar.activation(out=res[:, 2, :], in_=res[:, 2, :], func=RELU)
-            for first in (0, 2):
-                tiles = slice(block * BLOCK_TILES + first, block * BLOCK_TILES + first + 2)
-                nc.sync.dma_start(out=out_rows[:, tiles, n * BLK : (n + 1) * BLK], in_=res[:, first : first + 2, :])
+        def relu(unit, first, count, engine):
+            res = out_tiles[unit][:, first : first + count, :]
+            if engine == "V":
+                nc.vector.tensor_scalar_max(out=res, in0=res, scalar1=0.0)
+            elif engine == "G":
+                nc.gpsimd.tensor_scalar(out=res, in0=res, scalar1=0.0, scalar2=0.0, op0=MAX, op1=ADD)
+            else:
+                nc.scalar.activation(out=res, in_=res, func=RELU)
 
-        for half in range(X_LEAD):
-            transpose_x(half)
-            group_x(half)
-            quantise_x(half)
-        transpose_x(X_LEAD)
+        def store(unit, first, count):
+            block, n = divmod(unit, CHUNKS)
+            tiles = slice(block * BLOCK_TILES + first, block * BLOCK_TILES + first + count)
+            nc.sync.dma_start(out=out_rows[:, tiles, n * BLK : (n + 1) * BLK], in_=out_tiles[unit][:, first : first + count, :])
+
+        warm_up(6)
+        transpose_x(0)
+        transpose_x(1)
+        group_x(0, "V")
+        group_x(1, "S")
+        quantise_x(0, SIDES[0])
+        spread_b1()
+        quantise_x(0, SIDES[1])
+        for t in range(3):
+            hidden(0, t, WHOLE)
+        transpose_x(2, True)
+        group_x(2, "V")
+        transpose_x(3)
+        group_x(3, "V")
+        hidden(0, 3, WHOLE)
+        transpose_wb(0, 0, True)
+        quantise_x(1, WHOLE)
+        hidden(1, 0, WHOLE)
+        transpose_wb(0, 1, True)
+        hidden(1, 1, WHOLE)
+        group_h(0, WHOLE, "G")
+        leave_wb(0, 0, "V")
+        leave_wb(0, 1, "V")
+        transpose_x(4)
+        hidden(1, 2, WHOLE)
+        hidden(1, 3, WHOLE)
+        group_x(4, "V")
+        quantise_wb(0)
         nc.vector.tensor_copy(out=bb_all[:], in_=bb_bf16[:])
-        for step in range(UNITS + 3):
-            half = step + X_LEAD
-            if 0 <= step - 1 < UNITS:
-                group_h(step - 1)
-            if half < HALVES:
-                group_x(half)
-            if 0 <= step - 1 < CHUNKS:
-                transpose_wb(step - 1)
-            for i in range(PACK):
-                if 0 <= step - 2 < UNITS:
-                    second_matmul(step - 2, i)
-                if step < UNITS:
-                    first_matmul(step, i)
-                    leave_h(step, i)
+        quantise_h(0, WHOLE)
+        for t in range(PACK):
+            hidden(2, t, WHOLE)
+        transpose_x(5)
+        group_x(5, "V")
+        transpose_wb(1, 0)
+        leave_wb(1, 0, "S")
+        for unit in range(UNITS):
+            half = unit + 5
+            ahead = unit + 3
+            if unit + 1 < UNITS:
+                group_h(unit + 1, WHOLE, "G")
+            if unit == 0:
+                transpose_wb(1, 1)
+                leave_wb(1, 1, "S")
+            if unit >= 1:
+                u = unit - 1
+                relu(u, 0, 3, "S")
+                store(u, 0, 2)
+            m = 0
+            t = 0
+            for token in "mhmhmhmhTd":
+                if token == "m":
+                    second_matmul(unit, m)
+                    m += 1
+                elif token == "h":
+                    if ahead < UNITS:
+                        hidden(ahead, t, WHOLE)
+                    t += 1
+                elif token == "d":
+                    warm_up(1)
+                elif half + 1 < HALVES:
+                    transpose_x(half + 1)
+            if unit + 1 < UNITS:
+                quantise_h(unit + 1, WHOLE)
+            if half < HALVES and half % 2:
+                quantise_x(half // 2, WHOLE)
+            if unit == 0:
+                quantise_wb(1)
+            if unit >= 1:
+                relu(unit - 1, 3, 1, "V" if unit < 13 else "S")
+                store(unit - 1, 2, 2)
             if half + 1 < HALVES:
-                transpose_x(half + 1)
-            if 0 <= step - 1 < UNITS:
-                quantise_h(step - 1)
-            if 0 <= step - 1 < CHUNKS:
-                quantise_wb(step - 1)
-            if half < HALVES:
-                quantise_x(half)
-            if 0 <= step - 3 < UNITS:
-                relu_and_store(step - 3)
+                group_x(half + 1, "V")
+        u = UNITS - 1
+        for j in range(4):
+            relu(u, j, 1, "S")
+            if j % 2:
+                store(u, j - 1, 2)

@@ -56,7 +56,6 @@ def tile_blockdiagmnistconvertible_pa_t_kernel(tc, x, W1_words, W1_scales, b1, W
         b1_rows = keep.tile([P, P], BF16)
         b1_col = keep.tile([P, HID_TILES], F32)
         bb_bf16 = keep.tile([P, HID], BF16)
-        bb_all = keep.tile([P, HID], F32)
         ident_f32 = keep.tile([P, P], F32)
         ident_bf16 = keep.tile([P, P], BF16)
 
@@ -85,19 +84,19 @@ def tile_blockdiagmnistconvertible_pa_t_kernel(tc, x, W1_words, W1_scales, b1, W
 
         load_x(0)
         load_x(1)
+        load_x(2)
         for quadrant in range(4):
             nc.sync.dma_start(
                 out=w_scales[32 * quadrant : 32 * quadrant + 4, :].bitcast(I32),
                 in_=W1_scales[0, 4 * quadrant : 4 * quadrant + 4, :].bitcast(I32),
             )
         load_w(0)
-        load_x(2)
         load_x(3)
         load_wb(0)
         load_w(1)
         load_x(4)
-        nc.sync.dma_start(out=bb_bf16[:], in_=bb.partition_broadcast(P))
         load_wb(1)
+        nc.sync.dma_start(out=bb_bf16[:], in_=bb.partition_broadcast(P))
         for half in range(5, HALVES):
             load_x(half)
         nc.scalar.dma_start(out=b1_rows[0:HID_TILES, :], in_=b1.rearrange("(m p) -> m p", p=P))
@@ -233,7 +232,7 @@ def tile_blockdiagmnistconvertible_pa_t_kernel(tc, x, W1_words, W1_scales, b1, W
                 in_=h_grouped[unit][:, first:last, :].rearrange("p c t -> p (c t)"),
             )
 
-        def second_matmul(unit, j):
+        def second_matmul(unit, j, parts=1):
             n = unit % CHUNKS
             if unit not in out_tiles:
                 res = results.tile([P, BLOCK_TILES, BLK], F32)
@@ -249,7 +248,14 @@ def tile_blockdiagmnistconvertible_pa_t_kernel(tc, x, W1_words, W1_scales, b1, W
                 start=True,
                 stop=True,
             )
-            nc.vector.tensor_tensor(out=out_tiles[unit][:, j, :], in0=acc[:], in1=bb_all[:, n * BLK : (n + 1) * BLK], op=ADD)
+            width = BLK // parts
+            for first in range(0, BLK, width):
+                nc.vector.tensor_tensor(
+                    out=out_tiles[unit][:, j, first : first + width],
+                    in0=acc[:, first : first + width],
+                    in1=bb_bf16[:, n * BLK + first : n * BLK + first + width],
+                    op=ADD,
+                )
 
         def relu(unit, first, count, engine):
             res = out_tiles[unit][:, first : first + count, :]
@@ -260,71 +266,87 @@ def tile_blockdiagmnistconvertible_pa_t_kernel(tc, x, W1_words, W1_scales, b1, W
             else:
                 nc.scalar.activation(out=res, in_=res, func=RELU)
 
+        def finish(unit, j, parts):
+            block, n = divmod(unit, CHUNKS)
+            width = BLK // parts
+            for first in range(0, BLK, width):
+                res = out_tiles[unit][:, j, first : first + width]
+                nc.scalar.activation(out=res, in_=res, func=RELU)
+                nc.sync.dma_start(
+                    out=out_rows[:, block * BLOCK_TILES + j, n * BLK + first : n * BLK + first + width], in_=res
+                )
+
         def store(unit, first, count):
             block, n = divmod(unit, CHUNKS)
             tiles = slice(block * BLOCK_TILES + first, block * BLOCK_TILES + first + count)
             nc.sync.dma_start(out=out_rows[:, tiles, n * BLK : (n + 1) * BLK], in_=out_tiles[unit][:, first : first + count, :])
 
-        warm_up(6)
+        warm_up(4)
+        pending = [(unit, t) for unit in range(UNITS) for t in range(PACK)]
+
+        def next_hidden(count):
+            for i in range(count):
+                if pending:
+                    unit, t = pending[0]
+                    pending.remove(pending[0])
+                    hidden(unit, t, WHOLE)
+
         transpose_x(0)
         transpose_x(1)
         group_x(0, "V")
         group_x(1, "S")
         quantise_x(0, SIDES[0])
         spread_b1()
-        quantise_x(0, SIDES[1])
-        for t in range(3):
-            hidden(0, t, WHOLE)
         transpose_x(2, True)
+        quantise_x(0, SIDES[1])
         group_x(2, "V")
+        next_hidden(3)
         transpose_x(3)
+        next_hidden(1)
         group_x(3, "V")
-        hidden(0, 3, WHOLE)
         transpose_wb(0, 0, True)
-        quantise_x(1, WHOLE)
-        hidden(1, 0, WHOLE)
-        transpose_wb(0, 1, True)
-        hidden(1, 1, WHOLE)
-        group_h(0, WHOLE, "G")
         leave_wb(0, 0, "V")
-        leave_wb(0, 1, "V")
+        next_hidden(1)
+        transpose_wb(0, 1, True)
+        leave_wb(0, 1, "S")
+        group_h(0, WHOLE, "G")
+        next_hidden(1)
         transpose_x(4)
-        hidden(1, 2, WHOLE)
-        hidden(1, 3, WHOLE)
         group_x(4, "V")
+        next_hidden(1)
         quantise_wb(0)
-        nc.vector.tensor_copy(out=bb_all[:], in_=bb_bf16[:])
         quantise_h(0, WHOLE)
-        for t in range(PACK):
-            hidden(2, t, WHOLE)
+        next_hidden(1)
+        transpose_wb(1, 0, True)
+        quantise_x(1, WHOLE)
+        leave_wb(1, 0, "V")
         transpose_x(5)
+        next_hidden(2)
+        transpose_wb(1, 1)
+        leave_wb(1, 1, "S")
         group_x(5, "V")
-        transpose_wb(1, 0)
-        leave_wb(1, 0, "S")
+        LATE = 13
         for unit in range(UNITS):
             half = unit + 5
-            ahead = unit + 3
             if unit + 1 < UNITS:
                 group_h(unit + 1, WHOLE, "G")
-            if unit == 0:
-                transpose_wb(1, 1)
-                leave_wb(1, 1, "S")
-            if unit >= 1:
-                u = unit - 1
-                relu(u, 0, 3, "S")
-                store(u, 0, 2)
+            if 1 <= unit <= LATE:
+                some = 2 if half % 2 == 0 else 3
+                relu(unit - 1, 0, some, "S")
+                store(unit - 1, 0, 2)
             m = 0
-            t = 0
             for token in "mhmhmhmhTd":
                 if token == "m":
-                    second_matmul(unit, m)
+                    parts = 2 if unit == UNITS - 1 and m == 3 else 1
+                    second_matmul(unit, m, parts)
+                    if unit >= LATE:
+                        finish(unit, m, parts)
                     m += 1
                 elif token == "h":
-                    if ahead < UNITS:
-                        hidden(ahead, t, WHOLE)
-                    t += 1
+                    next_hidden(1)
                 elif token == "d":
-                    warm_up(1)
+                    if unit < 16:
+                        warm_up(1)
                 elif half + 1 < HALVES:
                     transpose_x(half + 1)
             if unit + 1 < UNITS:
@@ -333,13 +355,8 @@ def tile_blockdiagmnistconvertible_pa_t_kernel(tc, x, W1_words, W1_scales, b1, W
                 quantise_x(half // 2, WHOLE)
             if unit == 0:
                 quantise_wb(1)
-            if unit >= 1:
-                relu(unit - 1, 3, 1, "V" if unit < 13 else "S")
+            if 1 <= unit <= LATE:
+                relu(unit - 1, some, 4 - some, "V")
                 store(unit - 1, 2, 2)
             if half + 1 < HALVES:
-                group_x(half + 1, "V")
-        u = UNITS - 1
-        for j in range(4):
-            relu(u, j, 1, "S")
-            if j % 2:
-                store(u, j - 1, 2)
+                group_x(half + 1, "S" if half % 2 == 0 else "V")

@@ -210,8 +210,8 @@ def tile_blockdiagmnistconvertible_pa_t_kernel(tc, x, W1_words, W1_scales, b1, W
                 hg = work.tile([P, BLOCK, PACK], BF16, align_bytes=64, bufs=1)
                 h_grouped[unit] = hg
             first, last = span
-            dst = h_grouped[unit][:, first:last, :].rearrange("p (c i) t -> p c t i", i=4)
-            src = h_planes[unit][:, :, first:last].rearrange("p t (c i) -> p c t i", i=4)
+            dst = h_grouped[unit][:, first:last, :].rearrange("p (c i) t -> p c t i", i=8)
+            src = h_planes[unit][:, :, first:last].rearrange("p t (c i) -> p c t i", i=8)
             if engine == "G":
                 nc.gpsimd.tensor_scalar(out=dst, in0=src, scalar1=1.0, scalar2=0.0, op0=MULT, op1=ADD)
             elif engine == "V":

from contextlib import ExitStack

import concourse.mybir as mybir
from concourse.masks import make_identity

F32 = mybir.dt.float32
BF16 = mybir.dt.bfloat16
I32 = mybir.dt.int32
U32 = mybir.dt.uint32
U8 = mybir.dt.uint8
FP8X4 = mybir.dt.float8_e4m3fn_x4
RELU = mybir.ActivationFunctionType.Relu
ADD = mybir.AluOpType.add
MULT = mybir.AluOpType.mult
MAX = mybir.AluOpType.max

P = 128
PACK = 4
BATCH, IN, HID, BLK = 4096, 512, 1024, 512
CHUNKS = HID // BLK
ROW_TILES = BATCH // P
BLOCK_TILES = 4
BLOCK = BLOCK_TILES * P
BLOCKS = ROW_TILES // BLOCK_TILES
UNITS = BLOCKS * CHUNKS
HALF = BLOCK // 2
HALVES = 2 * BLOCKS
X_LEAD = 2
HID_TILES = HID // P
BANK = 512

FLOPS = 2 * BATCH * IN * HID + 2 * BATCH * HID * BLK


def tile_blockdiagmnistconvertible_pa_t_kernel(tc, x, W1_words, W1_scales, b1, Wb, bb, out):
    nc = tc.nc
    x_rows = x.rearrange("(p j) k -> p j k", j=ROW_TILES)
    out_rows = out.rearrange("(p j) o -> p j o", j=ROW_TILES)

    with ExitStack() as ctx:
        keep = ctx.enter_context(tc.tile_pool(name="keep", bufs=1))
        work = ctx.enter_context(tc.tile_pool(name="work", bufs=2))
        results = ctx.enter_context(tc.tile_pool(name="results", bufs=4))
        psum_t = ctx.enter_context(tc.psum_pool(name="psum_t", bufs=2))
        psum_h = ctx.enter_context(tc.psum_pool(name="psum_h", bufs=3))
        psum_y = ctx.enter_context(tc.psum_pool(name="psum_y", bufs=3))
        ctx.enter_context(tc.manual_schedule())

        x_sb = keep.tile([P, ROW_TILES, IN], BF16)
        w_words = keep.tile([P, HID], U32, align_bytes=64)
        w_scales = keep.tile([P, HID], U8, align_bytes=64)
        wb_sb = keep.tile([P, CHUNKS * BLOCK_TILES, BLK], BF16)
        wb_grouped = keep.tile([P, CHUNKS, BLK, PACK], BF16, align_bytes=64)
        wb_words = keep.tile([P, CHUNKS, BLK], U32, align_bytes=64)
        wb_scales = keep.tile([P, CHUNKS, BLK], U8, align_bytes=64)
        b1_rows = keep.tile([P, P], BF16)
        b1_col = keep.tile([P, HID_TILES], F32)
        bb_bf16 = keep.tile([P, HID], BF16)
        ident_f32 = keep.tile([P, P], F32)
        ident_bf16 = keep.tile([P, P], BF16)

        zeros = keep.tile([P, BANK], BF16)
        nc.vector.memset(zeros[:], 0.0)
        warm = keep.tile([P, 1], F32)
        nc.vector.memset(warm[:], 0.0)
        nc.vector.memset(w_scales[:].bitcast(I32), 0)
        nc.vector.memset(b1_rows[:], 0.0)

        def load_x(half):
            tiles = slice(2 * half, 2 * half + 2)
            nc.sync.dma_start(out=x_sb[:, tiles, :], in_=x_rows[:, tiles, :])

        def load_wb(n):
            nc.sync.dma_start(
                out=wb_sb[:, n * BLOCK_TILES : (n + 1) * BLOCK_TILES, :], in_=Wb[n].rearrange("(a p) k -> p a k", p=P)
            )

        def load_w(n):
            cols = slice(n * BLK, (n + 1) * BLK)
            nc.sync.dma_start(
                out=w_words[:, cols].bitcast(I32),
                in_=W1_words[0].rearrange("p n t -> p (n t)")[:, n * BLK * PACK : (n + 1) * BLK * PACK].bitcast(I32),
            )

        load_x(0)
        load_x(1)
        load_x(2)
        for quadrant in range(4):
            nc.sync.dma_start(
                out=w_scales[32 * quadrant : 32 * quadrant + 4, :].bitcast(I32),
                in_=W1_scales[0, 4 * quadrant : 4 * quadrant + 4, :].bitcast(I32),
            )
        load_w(0)
        load_x(3)
        load_wb(0)
        load_w(1)
        load_x(4)
        load_wb(1)
        nc.sync.dma_start(out=bb_bf16[:], in_=bb.partition_broadcast(P))
        for half in range(5, HALVES):
            load_x(half)
        nc.scalar.dma_start(out=b1_rows[0:HID_TILES, :], in_=b1.rearrange("(m p) -> m p", p=P))

        make_identity(nc, ident_f32[:])
        make_identity(nc, ident_bf16[:])
        nc.scalar.activation(out=warm[:], in_=warm[:], func=RELU)


        x_banks = {}
        x_grouped = {}
        x_codes = {}
        wb_banks = {}
        h_planes = {}
        h_grouped = {}
        h_codes = {}
        out_tiles = {}
        WHOLE = (0, BLOCK)
        SIDES = ((0, HALF), (HALF, BLOCK))

        def spread_b1():
            b1_t = psum_t.tile([P, P], BF16, tag="t")
            nc.tensor.transpose(b1_t[:], b1_rows[:], ident_bf16[:])
            nc.vector.tensor_copy(out=b1_col[:], in_=b1_t[:, 0:HID_TILES])

        def warm_up(count):
            for i in range(count):
                idle = psum_t.tile([P, BANK], F32, tag="t")
                nc.tensor.matmul(idle[:], lhsT=zeros[:, 0:P], rhs=zeros[:], start=True, stop=True)

        def transpose_x(half, early=False):
            pool, tag = (psum_y, "y") if early else (psum_t, "t")
            xt = pool.tile([P, 2, HALF], F32, tag=tag)
            for pair in range(2):
                words = x_sb[:, 2 * half + pair, :].bitcast(F32)
                for u in range(2):
                    nc.tensor.transpose(xt[:, u, pair * P : (pair + 1) * P], words[:, u : IN // 2 : 2], ident_f32[:])
            x_banks[half] = xt

        def group_x(half, engine):
            block, side = divmod(half, 2)
            if side == 0:
                xg = work.tile([P, BLOCK * PACK], BF16, align_bytes=64, bufs=2)
                x_grouped[block] = xg
            xg = x_grouped[block][:, side * HALF * PACK : (side + 1) * HALF * PACK]
            copy = nc.vector.tensor_copy if engine == "V" else nc.scalar.copy
            copy(
                out=xg.bitcast(F32).rearrange("p (c u) -> p c u", u=2),
                in_=x_banks[half][:].rearrange("p u c -> p c u"),
            )

        def quantise_x(block, span):
            if block not in x_codes:
                xq = work.tile([P, BLOCK], U32, align_bytes=64, bufs=3)
                xs = work.tile([P, BLOCK], U8, align_bytes=64, bufs=3)
                x_codes[block] = (xq, xs)
            xq, xs = x_codes[block]
            first, last = span
            nc.vector.quantize_mx(
                out=xq[:, first:last].bitcast(FP8X4), scales=xs[:, first:last], in_=x_grouped[block][:, first * PACK : last * PACK]
            )

        def transpose_wb(n, side, early=False):
            pool, tag = (psum_y, "y") if early else (psum_t, "t")
            wt = pool.tile([P, 2, PACK, P], BF16, tag=tag)
            for a in range(2):
                for t in range(PACK):
                    nc.tensor.transpose(
                        wt[:, a, t, :],
                        wb_sb[:, n * BLOCK_TILES + 2 * side + a, t * P : (t + 1) * P],
                        ident_bf16[:],
                    )
            wb_banks[(n, side)] = wt

        def leave_wb(n, side, engine):
            dst = wb_grouped[:, n, 2 * side * P : 2 * (side + 1) * P, :].rearrange("p (a o) t -> p a o t", a=2)
            copy = nc.vector.tensor_copy if engine == "V" else nc.scalar.copy
            copy(out=dst, in_=wb_banks[(n, side)][:].rearrange("p a t o -> p a o t"))

        def quantise_wb(n):
            nc.vector.quantize_mx(
                out=wb_words[:, n, :].bitcast(FP8X4),
                scales=wb_scales[:, n, :],
                in_=wb_grouped[:, n, :, :].rearrange("p o t -> p (o t)"),
            )

        def hidden(unit, t, span):
            block, n = divmod(unit, CHUNKS)
            m = n * PACK + t
            xq, xs = x_codes[block]
            first, last = span
            acc = psum_h.tile([P, BANK], F32)
            nc.tensor.matmul_mx(
                out=acc[:, 0 : last - first],
                lhsT=w_words[:, m * P : (m + 1) * P].bitcast(FP8X4),
                lhsT_scale=w_scales[:, m * P : (m + 1) * P],
                rhs=xq[:, first:last].bitcast(FP8X4),
                rhs_scale=xs[:, first:last],
                start=True,
                stop=True,
            )
            if unit not in h_planes:
                planes = work.tile([P, PACK, BLOCK], BF16, bufs=3)
                h_planes[unit] = planes
            nc.scalar.activation(
                out=h_planes[unit][:, t, first:last], in_=acc[:, 0 : last - first], func=RELU, bias=b1_col[:, m : m + 1], scale=1.0
            )

        def group_h(unit, span, engine):
            if unit not in h_grouped:
                hg = work.tile([P, BLOCK, PACK], BF16, align_bytes=64, bufs=1)
                h_grouped[unit] = hg
            first, last = span
            dst = h_grouped[unit][:, first:last, :].rearrange("p (c i) t -> p c t i", i=8)
            src = h_planes[unit][:, :, first:last].rearrange("p t (c i) -> p c t i", i=8)
            if engine == "G":
                nc.gpsimd.tensor_scalar(out=dst, in0=src, scalar1=1.0, scalar2=0.0, op0=MULT, op1=ADD)
            elif engine == "V":
                nc.vector.tensor_copy(out=dst, in_=src)
            else:
                nc.scalar.copy(out=dst, in_=src)

        def quantise_h(unit, span):
            if unit not in h_codes:
                hq = work.tile([P, BLOCK], U32, align_bytes=64, bufs=2)
                hs = work.tile([P, BLOCK], U8, align_bytes=64, bufs=2)
                h_codes[unit] = (hq, hs)
            hq, hs = h_codes[unit]
            first, last = span
            nc.vector.quantize_mx(
                out=hq[:, first:last].bitcast(FP8X4),
                scales=hs[:, first:last],
                in_=h_grouped[unit][:, first:last, :].rearrange("p c t -> p (c t)"),
            )

        def second_matmul(unit, j, parts=1):
            n = unit % CHUNKS
            if unit not in out_tiles:
                res = results.tile([P, BLOCK_TILES, BLK], F32)
                out_tiles[unit] = res
            hq, hs = h_codes[unit]
            acc = psum_y.tile([P, BANK], F32, tag="y")
            nc.tensor.matmul_mx(
                out=acc[:],
                lhsT=hq[:, j * P : (j + 1) * P].bitcast(FP8X4),
                lhsT_scale=hs[:, j * P : (j + 1) * P],
                rhs=wb_words[:, n, :].bitcast(FP8X4),
                rhs_scale=wb_scales[:, n, :],
                start=True,
                stop=True,
            )
            width = BLK // parts
            for first in range(0, BLK, width):
                nc.vector.tensor_tensor(
                    out=out_tiles[unit][:, j, first : first + width],
                    in0=acc[:, first : first + width],
                    in1=bb_bf16[:, n * BLK + first : n * BLK + first + width],
                    op=ADD,
                )

        def relu(unit, first, count, engine):
            res = out_tiles[unit][:, first : first + count, :]
            if engine == "V":
                nc.vector.tensor_scalar_max(out=res, in0=res, scalar1=0.0)
            elif engine == "G":
                nc.gpsimd.tensor_scalar(out=res, in0=res, scalar1=0.0, scalar2=0.0, op0=MAX, op1=ADD)
            else:
                nc.scalar.activation(out=res, in_=res, func=RELU)

        def finish(unit, j, parts):
            block, n = divmod(unit, CHUNKS)
            width = BLK // parts
            for first in range(0, BLK, width):
                res = out_tiles[unit][:, j, first : first + width]
                nc.scalar.activation(out=res, in_=res, func=RELU)
                nc.sync.dma_start(
                    out=out_rows[:, block * BLOCK_TILES + j, n * BLK + first : n * BLK + first + width], in_=res
                )

        def store(unit, first, count):
            block, n = divmod(unit, CHUNKS)
            tiles = slice(block * BLOCK_TILES + first, block * BLOCK_TILES + first + count)
            nc.sync.dma_start(out=out_rows[:, tiles, n * BLK : (n + 1) * BLK], in_=out_tiles[unit][:, first : first + count, :])

        warm_up(4)
        pending = [(unit, t) for unit in range(UNITS) for t in range(PACK)]

        def next_hidden(count):
            for i in range(count):
                if pending:
                    unit, t = pending[0]
                    pending.remove(pending[0])
                    hidden(unit, t, WHOLE)

        transpose_x(0)
        transpose_x(1)
        group_x(0, "V")
        group_x(1, "S")
        quantise_x(0, SIDES[0])
        spread_b1()
        transpose_x(2, True)
        quantise_x(0, SIDES[1])
        group_x(2, "V")
        next_hidden(3)
        transpose_x(3)
        next_hidden(1)
        group_x(3, "V")
        transpose_wb(0, 0, True)
        leave_wb(0, 0, "V")
        next_hidden(1)
        transpose_wb(0, 1, True)
        leave_wb(0, 1, "S")
        group_h(0, WHOLE, "G")
        next_hidden(1)
        transpose_x(4)
        group_x(4, "V")
        next_hidden(1)
        quantise_wb(0)
        quantise_h(0, WHOLE)
        next_hidden(1)
        transpose_wb(1, 0, True)
        quantise_x(1, WHOLE)
        leave_wb(1, 0, "V")
        transpose_x(5)
        next_hidden(2)
        transpose_wb(1, 1)
        leave_wb(1, 1, "S")
        group_x(5, "V")
        LATE = 13
        for unit in range(UNITS):
            half = unit + 5
            if unit + 1 < UNITS:
                group_h(unit + 1, WHOLE, "G")
            if 1 <= unit <= LATE:
                some = 2 if half % 2 == 0 else 3
                relu(unit - 1, 0, some, "S")
                store(unit - 1, 0, 2)
            m = 0
            for token in "mhmhmhmhTd":
                if token == "m":
                    parts = 2 if unit == UNITS - 1 and m == 3 else 1
                    second_matmul(unit, m, parts)
                    if unit >= LATE:
                        finish(unit, m, parts)
                    m += 1
                elif token == "h":
                    next_hidden(1)
                elif token == "d":
                    if unit < 16:
                        warm_up(1)
                elif half + 1 < HALVES:
                    transpose_x(half + 1)
            if unit + 1 < UNITS:
                quantise_h(unit + 1, WHOLE)
            if half < HALVES and half % 2:
                quantise_x(half // 2, WHOLE)
            if unit == 0:
                quantise_wb(1)
            if 1 <= unit <= LATE:
                relu(unit - 1, some, 4 - some, "V")
                store(unit - 1, 2, 2)
            if half + 1 < HALVES:
                group_x(half + 1, "S" if half % 2 == 0 else "V")
